import numpy as np
import ml_dtypes


def mxq(x, axis, fmt="e4m3"):
    dtype, down = {"e4m3": (ml_dtypes.float8_e4m3fn, 7), "e5m2": (ml_dtypes.float8_e5m2, 14)}[fmt]
    v = np.moveaxis(np.asarray(x, np.float32).astype(ml_dtypes.bfloat16).astype(np.float64), axis, -1)
    blocks = v.reshape(v.shape[:-1] + (-1, 32))
    amax = np.abs(blocks).max(-1, keepdims=True)
    byte = np.maximum(np.where(amax > 0, np.frexp(amax)[1] - 1 + 127, 0) - down, 1)
    scale = np.exp2(byte - 127.0)
    codes = (blocks / scale).astype(np.float32).astype(dtype).astype(np.float64)
    return np.moveaxis((codes * scale).reshape(v.shape), -1, axis)


WIDE = False


def mx_kscale(k):
    if not WIDE:
        return np.ones(k)
    levels = np.array([10, -10, 5, -5, 0])
    a = np.random.permutation(np.resize(levels, k // 512 * 4)).reshape(k // 512, 4)
    idx = np.arange(k)
    return np.exp2(a[idx // 512, idx % 128 // 32])


BF16 = ml_dtypes.bfloat16


def bf(x):
    return np.asarray(x, np.float32).astype(BF16)


def f64(x):
    return np.asarray(x).astype(np.float64)


B, S, D, DM, DK = 4, 1024, 512, 1024, 64
LN_EPS = 1e-5


def setup_inputs():
    s = mx_kscale(DM)
    return {
        "h_attn": bf(np.random.standard_normal((B, S, DM)) * 0.3 * s),
        "Wo": bf(np.random.standard_normal((DM, D)) * 3.0 / np.sqrt(DM) / s[:, None]),
        "bo": bf(np.random.standard_normal((B, S, D)) * 0.5 + np.random.uniform(0.25, 0.75, (B, 1, 1))),
        "x": bf(np.random.standard_normal((B, S, D))),
        "gamma": bf(1.0 + 0.1 * np.random.standard_normal((S, D))),
        "beta": bf(0.1 * np.random.standard_normal((S, D))),
    }


def reference(h_attn, Wo, bo, x, gamma, beta):
    o = (mxq(f64(h_attn), 2, "e4m3") @ mxq(f64(Wo), 0, "e4m3")) + f64(bo)
    o = o + f64(x)
    mu = o.mean(axis=(-2, -1), keepdims=True)
    var = np.square(o - mu).mean(axis=(-2, -1), keepdims=True)
    return (o - mu) / np.sqrt(var + LN_EPS) * f64(gamma) + f64(beta)

@@ -1,0 +1,260 @@
+from contextlib import ExitStack
+
+import concourse.mybir as mybir
+from concourse.masks import make_identity
+
+F32 = mybir.dt.float32
+BF16 = mybir.dt.bfloat16
+U32 = mybir.dt.uint32
+U8 = mybir.dt.uint8
+FP8X4 = mybir.dt.float8_e4m3fn_x4
+ADD = mybir.AluOpType.add
+MULT = mybir.AluOpType.mult
+FUNC = mybir.ActivationFunctionType
+
+P = 128
+BATCH, SEQ, K_DIM, D_OUT = 4, 1024, 1024, 512
+LN_EPS = 1e-5
+PACK = 4
+K_PASS = P * PACK
+PASSES = K_DIM // K_PASS
+TILES_PER_BATCH = SEQ // P
+CHUNK_TILES = 4
+CHUNKS_PER_BATCH = TILES_PER_BATCH // CHUNK_TILES
+CHUNKS = BATCH * CHUNKS_PER_BATCH
+CHUNK_K = CHUNK_TILES * K_DIM
+CHUNK_D = CHUNK_TILES * D_OUT
+BATCH_D = TILES_PER_BATCH * D_OUT
+WORDS = K_DIM // 2
+PLANES = WORDS // P
+TILE_CODES = K_DIM // PACK
+NORM_PIECES = 2
+PIECE_D = CHUNK_D // NORM_PIECES
+COUNT = SEQ * D_OUT
+
+PREFETCH = 4
+TRANSPOSE_AHEAD = 2
+QUANTISE_AHEAD = 1
+NORM_LAG = 4
+
+FLOPS = 2 * BATCH * SEQ * K_DIM * D_OUT
+
+
+def tile_multiheadattn_pb_t_kernel(tc, h_attn, Wo, bo, x, gamma, beta, out):
+    nc = tc.nc
+
+    h_view = h_attn.rearrange("b (p t) k -> p b (t k)", t=TILES_PER_BATCH)
+    bo_view = bo.rearrange("b (p t) d -> p b (t d)", t=TILES_PER_BATCH)
+    x_view = x.rearrange("b (p t) d -> p b (t d)", t=TILES_PER_BATCH)
+    out_view = out.rearrange("b (p t) d -> p b (t d)", t=TILES_PER_BATCH)
+    gamma_view = gamma.rearrange("(p t) d -> p (t d)", t=TILES_PER_BATCH)
+    beta_view = beta.rearrange("(p t) d -> p (t d)", t=TILES_PER_BATCH)
+    wo_view = Wo.rearrange("(a q e) c -> q a (e c)", a=PASSES * 2, e=2)
+
+    with ExitStack() as ctx:
+        const = ctx.enter_context(tc.tile_pool(name="const", bufs=1))
+        h_pool = ctx.enter_context(tc.tile_pool(name="h_pool", bufs=PREFETCH))
+        add_pool = ctx.enter_context(tc.tile_pool(name="add_pool", bufs=PREFETCH))
+        mx_pool = ctx.enter_context(tc.tile_pool(name="mx_pool", bufs=2))
+        scratch_pool = ctx.enter_context(tc.tile_pool(name="scratch_pool", bufs=2))
+        psum_xt = ctx.enter_context(tc.psum_pool(name="psum_xt", bufs=3))
+        psum_acc = ctx.enter_context(tc.psum_pool(name="psum_acc", bufs=CHUNK_TILES))
+        psum_stat = ctx.enter_context(tc.psum_pool(name="psum_stat", bufs=1))
+        ctx.enter_context(tc.manual_schedule())
+
+        ident = const.tile([P, P], F32)
+        make_identity(nc, ident[:])
+        ones = const.tile([P, P], F32)
+        nc.vector.memset(ones[:], 1.0)
+        eps = const.tile([P, 1], F32)
+        nc.vector.memset(eps[:], LN_EPS)
+
+        tile_sums = const.tile([P, BATCH * TILES_PER_BATCH], F32)
+        neg_mean = const.tile([P, BATCH], F32)
+        mean_scratch = const.tile([P, BATCH * TILES_PER_BATCH], F32)
+        square_sums = const.tile([P, BATCH], F32)
+        std = const.tile([P, BATCH], F32)
+        rstd = const.tile([P, BATCH], F32)
+
+        o_tiles = [const.tile([P, BATCH_D], F32, name="o%d" % b) for b in range(BATCH)]
+        gamma_sb = const.tile([P, BATCH_D], BF16)
+        beta_sb = const.tile([P, BATCH_D], BF16)
+
+        wo_raw = const.tile([P, PASSES * PACK * D_OUT], BF16)
+        wo_grouped = const.tile([P, PASSES * D_OUT * PACK], BF16, align_bytes=64)
+        wo_codes = const.tile([P, PASSES * D_OUT], U32, align_bytes=64)
+        wo_scales = const.tile([P, PASSES * D_OUT], U8, align_bytes=64)
+        nc.sync.dma_start(
+            out=wo_raw[:].rearrange("q (a r) -> q a r", a=PASSES * 2), in_=wo_view
+        )
+        wo_raw_gct = wo_raw[:].rearrange("q (g t c) -> q g c t", g=PASSES, t=PACK)
+        wo_grouped_gct = wo_grouped[:].rearrange("q (g c t) -> q g c t", g=PASSES, t=PACK)
+        for g in range(PASSES):
+            nc.vector.tensor_copy(out=wo_grouped_gct[:, g], in_=wo_raw_gct[:, g])
+        for g in range(PASSES):
+            nc.vector.quantize_mx(
+                out=wo_codes[:, g * D_OUT : (g + 1) * D_OUT].bitcast(FP8X4),
+                scales=wo_scales[:, g * D_OUT : (g + 1) * D_OUT],
+                in_=wo_grouped[:, g * D_OUT * PACK : (g + 1) * D_OUT * PACK],
+            )
+
+        h_in, bo_in, x_in = {}, {}, {}
+        h_grouped, h_codes, h_scales = {}, {}, {}
+        acc_of = {}
+
+        def chunk_cols(c, width):
+            half = c % CHUNKS_PER_BATCH
+            return slice(half * width, (half + 1) * width)
+
+        def load(c):
+            b = c // CHUNKS_PER_BATCH
+            h_sb = h_pool.tile([P, CHUNK_K], BF16)
+            nc.sync.dma_start(out=h_sb[:], in_=h_view[:, b, chunk_cols(c, CHUNK_K)])
+            bo_sb = add_pool.tile([P, CHUNK_D], BF16)
+            nc.sync.dma_start(out=bo_sb[:], in_=bo_view[:, b, chunk_cols(c, CHUNK_D)])
+            x_sb = add_pool.tile([P, CHUNK_D], BF16)
+            nc.sync.dma_start(out=x_sb[:], in_=x_view[:, b, chunk_cols(c, CHUNK_D)])
+            h_in[c], bo_in[c], x_in[c] = h_sb, bo_sb, x_sb
+
+        def transpose(c):
+            h_words = h_in[c][:].bitcast(F32)
+            grouped = mx_pool.tile([P, CHUNK_K], BF16, align_bytes=64)
+            grouped_words = grouped[:].bitcast(F32)
+            for j in range(CHUNK_TILES):
+                xt = psum_xt.tile([P, PLANES, P], F32)
+                for a in range(PLANES):
+                    first = (j * PLANES + a) * P
+                    nc.tensor.transpose(xt[:, a, :], h_words[:, first : first + P], ident[:])
+                nc.scalar.copy(
+                    out=grouped_words[:, j * WORDS : (j + 1) * WORDS].rearrange(
+                        "q (g r u) -> q g r u", g=PASSES, u=2
+                    ),
+                    in_=xt[:].rearrange("q (g u) r -> q g r u", g=PASSES),
+                )
+            h_grouped[c] = grouped
+
+        def quantise(c):
+            codes = mx_pool.tile([P, CHUNK_TILES * TILE_CODES], U32, align_bytes=64)
+            scales = mx_pool.tile([P, CHUNK_TILES * TILE_CODES], U8, align_bytes=64)
+            nc.vector.quantize_mx(
+                out=codes[:].bitcast(FP8X4), scales=scales[:], in_=h_grouped[c][:]
+            )
+            h_codes[c], h_scales[c] = codes, scales
+
+        def project(c):
+            for j in range(CHUNK_TILES):
+                acc = psum_acc.tile([P, D_OUT], F32)
+                for g in range(PASSES):
+                    tokens = slice((j * PASSES + g) * P, (j * PASSES + g + 1) * P)
+                    features = slice(g * D_OUT, (g + 1) * D_OUT)
+                    nc.tensor.matmul_mx(
+                        out=acc[:],
+                        lhsT=h_codes[c][:, tokens].bitcast(FP8X4),
+                        lhsT_scale=h_scales[c][:, tokens],
+                        rhs=wo_codes[:, features].bitcast(FP8X4),
+                        rhs_scale=wo_scales[:, features],
+                        start=(g == 0),
+                        stop=(g == PASSES - 1),
+                    )
+                acc_of[(c, j)] = acc
+
+        def add_bias_and_residual(c):
+            o_chunk = o_tiles[c // CHUNKS_PER_BATCH][:, chunk_cols(c, CHUNK_D)]
+            nc.vector.tensor_tensor(out=o_chunk, in0=bo_in[c][:], in1=x_in[c][:], op=ADD)
+
+        def add_projection(c):
+            o_chunk = o_tiles[c // CHUNKS_PER_BATCH][:, chunk_cols(c, CHUNK_D)]
+            for j in range(CHUNK_TILES):
+                o_tile = o_chunk[:, j * D_OUT : (j + 1) * D_OUT]
+                column = c * CHUNK_TILES + j
+                nc.vector.scalar_tensor_tensor(
+                    out=o_tile,
+                    in0=acc_of[(c, j)][:],
+                    scalar=0.0,
+                    in1=o_tile,
+                    op0=ADD,
+                    op1=ADD,
+                    accum_out=tile_sums[:, column : column + 1],
+                )
+
+        def mean_and_squares(b):
+            columns = slice(b * TILES_PER_BATCH, (b + 1) * TILES_PER_BATCH)
+            totals = psum_stat.tile([P, TILES_PER_BATCH], F32, tag="stat")
+            nc.tensor.matmul(totals[:], lhsT=ones[:], rhs=tile_sums[:, columns], start=True, stop=True)
+            nc.scalar.activation(
+                out=mean_scratch[:, columns],
+                in_=totals[:],
+                func=FUNC.Copy,
+                scale=-1.0 / COUNT,
+                accum_out=neg_mean[:, b : b + 1],
+            )
+            squares = scratch_pool.tile([P, BATCH_D], BF16)
+            nc.scalar.activation(
+                out=squares[:],
+                in_=o_tiles[b][:],
+                func=FUNC.Square,
+                bias=neg_mean[:, b : b + 1],
+                accum_out=square_sums[:, b : b + 1],
+            )
+
+        def standard_deviation(b):
+            total = psum_stat.tile([P, 1], F32, tag="stat")
+            nc.tensor.matmul(total[:], lhsT=ones[:], rhs=square_sums[:, b : b + 1], start=True, stop=True)
+            nc.scalar.activation(
+                out=std[:, b : b + 1], in_=total[:], func=FUNC.Sqrt, bias=eps[:], scale=1.0 / COUNT
+            )
+
+        def normalise_and_store(c):
+            b = c // CHUNKS_PER_BATCH
+            if c % CHUNKS_PER_BATCH == 0:
+                nc.vector.reciprocal(out=rstd[:, b : b + 1], in_=std[:, b : b + 1])
+            first = (c % CHUNKS_PER_BATCH) * CHUNK_D
+            pieces = [slice(first + n * PIECE_D, first + (n + 1) * PIECE_D) for n in range(NORM_PIECES)]
+            for piece in pieces:
+                nc.vector.scalar_tensor_tensor(
+                    out=o_tiles[b][:, piece],
+                    in0=o_tiles[b][:, piece],
+                    scalar=neg_mean[:, b : b + 1],
+                    in1=gamma_sb[:, piece],
+                    op0=ADD,
+                    op1=MULT,
+                )
+            for piece in pieces:
+                nc.vector.scalar_tensor_tensor(
+                    out=o_tiles[b][:, piece],
+                    in0=o_tiles[b][:, piece],
+                    scalar=rstd[:, b : b + 1],
+                    in1=beta_sb[:, piece],
+                    op0=MULT,
+                    op1=ADD,
+                )
+                nc.sync.dma_start(out=out_view[:, b, piece], in_=o_tiles[b][:, piece])
+
+        def is_chunk(c):
+            return 0 <= c < CHUNKS
+
+        for i in range(-PREFETCH, CHUNKS + NORM_LAG):
+            stats_batch = i // CHUNKS_PER_BATCH - 1
+            do_stats = i % CHUNKS_PER_BATCH == 0 and 0 <= stats_batch < BATCH
+
+            if is_chunk(i + PREFETCH):
+                load(i + PREFETCH)
+            if i == 0:
+                nc.sync.dma_start(out=gamma_sb[:], in_=gamma_view)
+                nc.sync.dma_start(out=beta_sb[:], in_=beta_view)
+            if is_chunk(i + TRANSPOSE_AHEAD):
+                transpose(i + TRANSPOSE_AHEAD)
+            if do_stats:
+                mean_and_squares(stats_batch)
+            if is_chunk(i + QUANTISE_AHEAD):
+                quantise(i + QUANTISE_AHEAD)
+            if is_chunk(i + TRANSPOSE_AHEAD):
+                add_bias_and_residual(i + TRANSPOSE_AHEAD)
+            if is_chunk(i):
+                add_projection(i)
+            if is_chunk(i + QUANTISE_AHEAD):
+                project(i + QUANTISE_AHEAD)
+            if do_stats:
+                standard_deviation(stats_batch)
+            if is_chunk(i - NORM_LAG):
+                normalise_and_store(i - NORM_LAG)

@@ -37,6 +37,8 @@ TRANSPOSE_AHEAD = 2
 QUANTISE_AHEAD = 1
 NORM_LAG = 4
 
+TENSOR_ADD_TILES = 3
+
 FLOPS = 2 * BATCH * SEQ * K_DIM * D_OUT
 
 
@@ -57,13 +59,15 @@ def tile_multiheadattn_pb_t_kernel(tc, h_attn, Wo, bo, x, gamma, beta, out):
         add_pool = ctx.enter_context(tc.tile_pool(name="add_pool", bufs=PREFETCH))
         mx_pool = ctx.enter_context(tc.tile_pool(name="mx_pool", bufs=2))
         scratch_pool = ctx.enter_context(tc.tile_pool(name="scratch_pool", bufs=2))
-        psum_xt = ctx.enter_context(tc.psum_pool(name="psum_xt", bufs=3))
+        psum_xt = ctx.enter_context(tc.psum_pool(name="psum_xt", bufs=2))
         psum_acc = ctx.enter_context(tc.psum_pool(name="psum_acc", bufs=CHUNK_TILES))
-        psum_stat = ctx.enter_context(tc.psum_pool(name="psum_stat", bufs=1))
+        psum_plain = ctx.enter_context(tc.psum_pool(name="psum_plain", bufs=2))
         ctx.enter_context(tc.manual_schedule())
 
         ident = const.tile([P, P], F32)
         make_identity(nc, ident[:])
+        ident_bf16 = const.tile([P, P], BF16)
+        make_identity(nc, ident_bf16[:])
         ones = const.tile([P, P], F32)
         nc.vector.memset(ones[:], 1.0)
         eps = const.tile([P, 1], F32)
@@ -84,9 +88,11 @@ def tile_multiheadattn_pb_t_kernel(tc, h_attn, Wo, bo, x, gamma, beta, out):
         wo_grouped = const.tile([P, PASSES * D_OUT * PACK], BF16, align_bytes=64)
         wo_codes = const.tile([P, PASSES * D_OUT], U32, align_bytes=64)
         wo_scales = const.tile([P, PASSES * D_OUT], U8, align_bytes=64)
-        nc.sync.dma_start(
-            out=wo_raw[:].rearrange("q (a r) -> q a r", a=PASSES * 2), in_=wo_view
-        )
+        wo_raw_halves = wo_raw[:].rearrange("q (a r) -> q a r", a=PASSES * 2)
+        for g in range(PASSES):
+            nc.sync.dma_start(
+                out=wo_raw_halves[:, 2 * g : 2 * g + 2, :], in_=wo_view[:, 2 * g : 2 * g + 2, :]
+            )
         wo_raw_gct = wo_raw[:].rearrange("q (g t c) -> q g c t", g=PASSES, t=PACK)
         wo_grouped_gct = wo_grouped[:].rearrange("q (g c t) -> q g c t", g=PASSES, t=PACK)
         for g in range(PASSES):
@@ -160,7 +166,18 @@ def tile_multiheadattn_pb_t_kernel(tc, h_attn, Wo, bo, x, gamma, beta, out):
 
         def add_bias_and_residual(c):
             o_chunk = o_tiles[c // CHUNKS_PER_BATCH][:, chunk_cols(c, CHUNK_D)]
-            nc.vector.tensor_tensor(out=o_chunk, in0=bo_in[c][:], in1=x_in[c][:], op=ADD)
+            first_tile = (c % CHUNKS_PER_BATCH) * CHUNK_TILES
+            vector_tiles = min(CHUNK_TILES, TILES_PER_BATCH - TENSOR_ADD_TILES - first_tile)
+            cols = slice(0, vector_tiles * D_OUT)
+            nc.vector.tensor_tensor(
+                out=o_chunk[:, cols], in0=bo_in[c][:, cols], in1=x_in[c][:, cols], op=ADD
+            )
+            for j in range(vector_tiles, CHUNK_TILES):
+                cols = slice(j * D_OUT, (j + 1) * D_OUT)
+                bx = psum_plain.tile([P, D_OUT], F32, tag="plain")
+                nc.tensor.matmul(bx[:], lhsT=ident_bf16[:], rhs=bo_in[c][:, cols], start=True, stop=False)
+                nc.tensor.matmul(bx[:], lhsT=ident_bf16[:], rhs=x_in[c][:, cols], start=False, stop=True)
+                nc.scalar.copy(out=o_chunk[:, cols], in_=bx[:])
 
         def add_projection(c):
             o_chunk = o_tiles[c // CHUNKS_PER_BATCH][:, chunk_cols(c, CHUNK_D)]
@@ -179,7 +196,7 @@ def tile_multiheadattn_pb_t_kernel(tc, h_attn, Wo, bo, x, gamma, beta, out):
 
         def mean_and_squares(b):
             columns = slice(b * TILES_PER_BATCH, (b + 1) * TILES_PER_BATCH)
-            totals = psum_stat.tile([P, TILES_PER_BATCH], F32, tag="stat")
+            totals = psum_plain.tile([P, TILES_PER_BATCH], F32, tag="plain")
             nc.tensor.matmul(totals[:], lhsT=ones[:], rhs=tile_sums[:, columns], start=True, stop=True)
             nc.scalar.activation(
                 out=mean_scratch[:, columns],
@@ -198,7 +215,7 @@ def tile_multiheadattn_pb_t_kernel(tc, h_attn, Wo, bo, x, gamma, beta, out):
             )
 
         def standard_deviation(b):
-            total = psum_stat.tile([P, 1], F32, tag="stat")
+            total = psum_plain.tile([P, 1], F32, tag="plain")
             nc.tensor.matmul(total[:], lhsT=ones[:], rhs=square_sums[:, b : b + 1], start=True, stop=True)
             nc.scalar.activation(
                 out=std[:, b : b + 1], in_=total[:], func=FUNC.Sqrt, bias=eps[:], scale=1.0 / COUNT

@@ -32,11 +32,10 @@ NORM_PIECES = 2
 PIECE_D = CHUNK_D // NORM_PIECES
 COUNT = SEQ * D_OUT
 
-PREFETCH = 4
-TRANSPOSE_AHEAD = 2
-QUANTISE_AHEAD = 1
-NORM_LAG = 4
+INPUT_BUFS = 4
+STAGE_BUFS = 3
 
+TENSOR_ADD_FROM = CHUNKS // 2
 TENSOR_ADD_TILES = 3
 
 FLOPS = 2 * BATCH * SEQ * K_DIM * D_OUT
@@ -55,14 +54,14 @@ def tile_multiheadattn_pb_t_kernel(tc, h_attn, Wo, bo, x, gamma, beta, out):
 
     with ExitStack() as ctx:
         const = ctx.enter_context(tc.tile_pool(name="const", bufs=1))
-        h_pool = ctx.enter_context(tc.tile_pool(name="h_pool", bufs=PREFETCH))
-        add_pool = ctx.enter_context(tc.tile_pool(name="add_pool", bufs=PREFETCH))
-        mx_pool = ctx.enter_context(tc.tile_pool(name="mx_pool", bufs=2))
-        scratch_pool = ctx.enter_context(tc.tile_pool(name="scratch_pool", bufs=2))
+        h_pool = ctx.enter_context(tc.tile_pool(name="h_pool", bufs=INPUT_BUFS))
+        add_pool = ctx.enter_context(tc.tile_pool(name="add_pool", bufs=INPUT_BUFS))
+        grouped_pool = ctx.enter_context(tc.tile_pool(name="grouped_pool", bufs=STAGE_BUFS))
+        mx_pool = ctx.enter_context(tc.tile_pool(name="mx_pool", bufs=STAGE_BUFS))
+        scratch_pool = ctx.enter_context(tc.tile_pool(name="scratch_pool", bufs=4))
         psum_xt = ctx.enter_context(tc.psum_pool(name="psum_xt", bufs=2))
         psum_acc = ctx.enter_context(tc.psum_pool(name="psum_acc", bufs=CHUNK_TILES))
         psum_plain = ctx.enter_context(tc.psum_pool(name="psum_plain", bufs=2))
-        ctx.enter_context(tc.manual_schedule())
 
         ident = const.tile([P, P], F32)
         make_identity(nc, ident[:])
@@ -76,7 +75,9 @@ def tile_multiheadattn_pb_t_kernel(tc, h_attn, Wo, bo, x, gamma, beta, out):
         tile_sums = const.tile([P, BATCH * TILES_PER_BATCH], F32)
         neg_mean = const.tile([P, BATCH], F32)
         mean_scratch = const.tile([P, BATCH * TILES_PER_BATCH], F32)
-        square_sums = const.tile([P, BATCH], F32)
+        square_sums = const.tile([P, BATCH * TILES_PER_BATCH], F32)
+        var_scratch = const.tile([P, BATCH * TILES_PER_BATCH], F32)
+        var = const.tile([P, BATCH], F32)
         std = const.tile([P, BATCH], F32)
         rstd = const.tile([P, BATCH], F32)
 
@@ -124,7 +125,7 @@ def tile_multiheadattn_pb_t_kernel(tc, h_attn, Wo, bo, x, gamma, beta, out):
 
         def transpose(c):
             h_words = h_in[c][:].bitcast(F32)
-            grouped = mx_pool.tile([P, CHUNK_K], BF16, align_bytes=64)
+            grouped = grouped_pool.tile([P, CHUNK_K], BF16, align_bytes=64)
             grouped_words = grouped[:].bitcast(F32)
             for j in range(CHUNK_TILES):
                 xt = psum_xt.tile([P, PLANES, P], F32)
@@ -166,8 +167,7 @@ def tile_multiheadattn_pb_t_kernel(tc, h_attn, Wo, bo, x, gamma, beta, out):
 
         def add_bias_and_residual(c):
             o_chunk = o_tiles[c // CHUNKS_PER_BATCH][:, chunk_cols(c, CHUNK_D)]
-            first_tile = (c % CHUNKS_PER_BATCH) * CHUNK_TILES
-            vector_tiles = min(CHUNK_TILES, TILES_PER_BATCH - TENSOR_ADD_TILES - first_tile)
+            vector_tiles = CHUNK_TILES if c < TENSOR_ADD_FROM else CHUNK_TILES - TENSOR_ADD_TILES
             cols = slice(0, vector_tiles * D_OUT)
             nc.vector.tensor_tensor(
                 out=o_chunk[:, cols], in0=bo_in[c][:, cols], in1=x_in[c][:, cols], op=ADD
@@ -194,7 +194,7 @@ def tile_multiheadattn_pb_t_kernel(tc, h_attn, Wo, bo, x, gamma, beta, out):
                     accum_out=tile_sums[:, column : column + 1],
                 )
 
-        def mean_and_squares(b):
+        def mean(b):
             columns = slice(b * TILES_PER_BATCH, (b + 1) * TILES_PER_BATCH)
             totals = psum_plain.tile([P, TILES_PER_BATCH], F32, tag="plain")
             nc.tensor.matmul(totals[:], lhsT=ones[:], rhs=tile_sums[:, columns], start=True, stop=True)
@@ -205,21 +205,32 @@ def tile_multiheadattn_pb_t_kernel(tc, h_attn, Wo, bo, x, gamma, beta, out):
                 scale=-1.0 / COUNT,
                 accum_out=neg_mean[:, b : b + 1],
             )
-            squares = scratch_pool.tile([P, BATCH_D], BF16)
+
+        def square_tile(c, j):
+            b = c // CHUNKS_PER_BATCH
+            first = (c % CHUNKS_PER_BATCH) * CHUNK_D + j * D_OUT
+            column = c * CHUNK_TILES + j
+            squares = scratch_pool.tile([P, D_OUT], BF16)
             nc.scalar.activation(
                 out=squares[:],
-                in_=o_tiles[b][:],
+                in_=o_tiles[b][:, first : first + D_OUT],
                 func=FUNC.Square,
                 bias=neg_mean[:, b : b + 1],
-                accum_out=square_sums[:, b : b + 1],
+                accum_out=square_sums[:, column : column + 1],
             )
 
         def standard_deviation(b):
-            total = psum_plain.tile([P, 1], F32, tag="plain")
-            nc.tensor.matmul(total[:], lhsT=ones[:], rhs=square_sums[:, b : b + 1], start=True, stop=True)
+            columns = slice(b * TILES_PER_BATCH, (b + 1) * TILES_PER_BATCH)
+            totals = psum_plain.tile([P, TILES_PER_BATCH], F32, tag="plain")
+            nc.tensor.matmul(totals[:], lhsT=ones[:], rhs=square_sums[:, columns], start=True, stop=True)
             nc.scalar.activation(
-                out=std[:, b : b + 1], in_=total[:], func=FUNC.Sqrt, bias=eps[:], scale=1.0 / COUNT
+                out=var_scratch[:, columns],
+                in_=totals[:],
+                func=FUNC.Copy,
+                scale=1.0 / COUNT,
+                accum_out=var[:, b : b + 1],
             )
+            nc.scalar.activation(out=std[:, b : b + 1], in_=var[:, b : b + 1], func=FUNC.Sqrt, bias=eps[:])
 
         def normalise_and_store(c):
             b = c // CHUNKS_PER_BATCH
@@ -250,28 +261,24 @@ def tile_multiheadattn_pb_t_kernel(tc, h_attn, Wo, bo, x, gamma, beta, out):
         def is_chunk(c):
             return 0 <= c < CHUNKS
 
-        for i in range(-PREFETCH, CHUNKS + NORM_LAG):
-            stats_batch = i // CHUNKS_PER_BATCH - 1
-            do_stats = i % CHUNKS_PER_BATCH == 0 and 0 <= stats_batch < BATCH
-
-            if is_chunk(i + PREFETCH):
-                load(i + PREFETCH)
-            if i == 0:
-                nc.sync.dma_start(out=gamma_sb[:], in_=gamma_view)
-                nc.sync.dma_start(out=beta_sb[:], in_=beta_view)
-            if is_chunk(i + TRANSPOSE_AHEAD):
-                transpose(i + TRANSPOSE_AHEAD)
-            if do_stats:
-                mean_and_squares(stats_batch)
-            if is_chunk(i + QUANTISE_AHEAD):
-                quantise(i + QUANTISE_AHEAD)
-            if is_chunk(i + TRANSPOSE_AHEAD):
-                add_bias_and_residual(i + TRANSPOSE_AHEAD)
-            if is_chunk(i):
-                add_projection(i)
-            if is_chunk(i + QUANTISE_AHEAD):
-                project(i + QUANTISE_AHEAD)
-            if do_stats:
-                standard_deviation(stats_batch)
-            if is_chunk(i - NORM_LAG):
-                normalise_and_store(i - NORM_LAG)
+        for c in range(INPUT_BUFS):
+            load(c)
+        nc.sync.dma_start(out=gamma_sb[:], in_=gamma_view)
+        nc.sync.dma_start(out=beta_sb[:], in_=beta_view)
+        for c in range(CHUNKS):
+            transpose(c)
+            quantise(c)
+            add_bias_and_residual(c)
+            project(c)
+            add_projection(c)
+            if is_chunk(c + INPUT_BUFS):
+                load(c + INPUT_BUFS)
+            if c % CHUNKS_PER_BATCH == CHUNKS_PER_BATCH - 1:
+                b = c // CHUNKS_PER_BATCH
+                mean(b)
+                for cc in range(c - CHUNKS_PER_BATCH + 1, c + 1):
+                    for j in range(CHUNK_TILES):
+                        square_tile(cc, j)
+                standard_deviation(b)
+        for c in range(CHUNKS):
+            normalise_and_store(c)

@@ -37,6 +37,8 @@ STAGE_BUFS = 3
 
 TENSOR_ADD_FROM = CHUNKS // 2
 TENSOR_ADD_TILES = 3
+GPSIMD_ADD_FROM = 3
+assert GPSIMD_ADD_FROM <= TENSOR_ADD_FROM
 
 FLOPS = 2 * BATCH * SEQ * K_DIM * D_OUT
 
@@ -167,12 +169,16 @@ def tile_multiheadattn_pb_t_kernel(tc, h_attn, Wo, bo, x, gamma, beta, out):
 
         def add_bias_and_residual(c):
             o_chunk = o_tiles[c // CHUNKS_PER_BATCH][:, chunk_cols(c, CHUNK_D)]
-            vector_tiles = CHUNK_TILES if c < TENSOR_ADD_FROM else CHUNK_TILES - TENSOR_ADD_TILES
-            cols = slice(0, vector_tiles * D_OUT)
-            nc.vector.tensor_tensor(
-                out=o_chunk[:, cols], in0=bo_in[c][:, cols], in1=x_in[c][:, cols], op=ADD
-            )
-            for j in range(vector_tiles, CHUNK_TILES):
+            plain_tiles = CHUNK_TILES if c < TENSOR_ADD_FROM else CHUNK_TILES - TENSOR_ADD_TILES
+            if c < GPSIMD_ADD_FROM:
+                nc.vector.tensor_tensor(out=o_chunk, in0=bo_in[c][:], in1=x_in[c][:], op=ADD)
+            else:
+                for j in range(plain_tiles):
+                    cols = slice(j * D_OUT, (j + 1) * D_OUT)
+                    nc.gpsimd.tensor_tensor(
+                        out=o_chunk[:, cols], in0=bo_in[c][:, cols], in1=x_in[c][:, cols], op=ADD
+                    )
+            for j in range(plain_tiles, CHUNK_TILES):
                 cols = slice(j * D_OUT, (j + 1) * D_OUT)
                 bx = psum_plain.tile([P, D_OUT], F32, tag="plain")
                 nc.tensor.matmul(bx[:], lhsT=ident_bf16[:], rhs=bo_in[c][:, cols], start=True, stop=False)

from contextlib import ExitStack

import concourse.mybir as mybir
from concourse.masks import make_identity

F32 = mybir.dt.float32
BF16 = mybir.dt.bfloat16
U32 = mybir.dt.uint32
U8 = mybir.dt.uint8
FP8X4 = mybir.dt.float8_e4m3fn_x4
ADD = mybir.AluOpType.add
MULT = mybir.AluOpType.mult
FUNC = mybir.ActivationFunctionType

P = 128
BATCH, SEQ, K_DIM, D_OUT = 4, 1024, 1024, 512
LN_EPS = 1e-5
PACK = 4
K_PASS = P * PACK
PASSES = K_DIM // K_PASS
TILES_PER_BATCH = SEQ // P
CHUNK_TILES = 4
CHUNKS_PER_BATCH = TILES_PER_BATCH // CHUNK_TILES
CHUNKS = BATCH * CHUNKS_PER_BATCH
CHUNK_K = CHUNK_TILES * K_DIM
CHUNK_D = CHUNK_TILES * D_OUT
BATCH_D = TILES_PER_BATCH * D_OUT
WORDS = K_DIM // 2
PLANES = WORDS // P
TILE_CODES = K_DIM // PACK
NORM_PIECES = 2
PIECE_D = CHUNK_D // NORM_PIECES
COUNT = SEQ * D_OUT

INPUT_BUFS = 4
STAGE_BUFS = 3

TENSOR_ADD_FROM = CHUNKS // 2
TENSOR_ADD_TILES = 3
GPSIMD_ADD_FROM = 3
assert GPSIMD_ADD_FROM <= TENSOR_ADD_FROM

FLOPS = 2 * BATCH * SEQ * K_DIM * D_OUT


def tile_multiheadattn_pb_t_kernel(tc, h_attn, Wo, bo, x, gamma, beta, out):
    nc = tc.nc

    h_view = h_attn.rearrange("b (p t) k -> p b (t k)", t=TILES_PER_BATCH)
    bo_view = bo.rearrange("b (p t) d -> p b (t d)", t=TILES_PER_BATCH)
    x_view = x.rearrange("b (p t) d -> p b (t d)", t=TILES_PER_BATCH)
    out_view = out.rearrange("b (p t) d -> p b (t d)", t=TILES_PER_BATCH)
    gamma_view = gamma.rearrange("(p t) d -> p (t d)", t=TILES_PER_BATCH)
    beta_view = beta.rearrange("(p t) d -> p (t d)", t=TILES_PER_BATCH)
    wo_view = Wo.rearrange("(a q e) c -> q a (e c)", a=PASSES * 2, e=2)

    with ExitStack() as ctx:
        const = ctx.enter_context(tc.tile_pool(name="const", bufs=1))
        h_pool = ctx.enter_context(tc.tile_pool(name="h_pool", bufs=INPUT_BUFS))
        add_pool = ctx.enter_context(tc.tile_pool(name="add_pool", bufs=INPUT_BUFS))
        grouped_pool = ctx.enter_context(tc.tile_pool(name="grouped_pool", bufs=STAGE_BUFS))
        mx_pool = ctx.enter_context(tc.tile_pool(name="mx_pool", bufs=STAGE_BUFS))
        scratch_pool = ctx.enter_context(tc.tile_pool(name="scratch_pool", bufs=4))
        psum_xt = ctx.enter_context(tc.psum_pool(name="psum_xt", bufs=2))
        psum_acc = ctx.enter_context(tc.psum_pool(name="psum_acc", bufs=CHUNK_TILES))
        psum_plain = ctx.enter_context(tc.psum_pool(name="psum_plain", bufs=2))

        ident = const.tile([P, P], F32)
        make_identity(nc, ident[:])
        ident_bf16 = const.tile([P, P], BF16)
        make_identity(nc, ident_bf16[:])
        ones = const.tile([P, P], F32)
        nc.vector.memset(ones[:], 1.0)
        eps = const.tile([P, 1], F32)
        nc.vector.memset(eps[:], LN_EPS)

        tile_sums = const.tile([P, BATCH * TILES_PER_BATCH], F32)
        neg_mean = const.tile([P, BATCH], F32)
        mean_scratch = const.tile([P, BATCH * TILES_PER_BATCH], F32)
        square_sums = const.tile([P, BATCH * TILES_PER_BATCH], F32)
        var_scratch = const.tile([P, BATCH * TILES_PER_BATCH], F32)
        var = const.tile([P, BATCH], F32)
        std = const.tile([P, BATCH], F32)
        rstd = const.tile([P, BATCH], F32)

        o_tiles = [const.tile([P, BATCH_D], F32, name="o%d" % b) for b in range(BATCH)]
        gamma_sb = const.tile([P, BATCH_D], BF16)
        beta_sb = const.tile([P, BATCH_D], BF16)

        wo_raw = const.tile([P, PASSES * PACK * D_OUT], BF16)
        wo_grouped = const.tile([P, PASSES * D_OUT * PACK], BF16, align_bytes=64)
        wo_codes = const.tile([P, PASSES * D_OUT], U32, align_bytes=64)
        wo_scales = const.tile([P, PASSES * D_OUT], U8, align_bytes=64)
        wo_raw_halves = wo_raw[:].rearrange("q (a r) -> q a r", a=PASSES * 2)
        for g in range(PASSES):
            nc.sync.dma_start(
                out=wo_raw_halves[:, 2 * g : 2 * g + 2, :], in_=wo_view[:, 2 * g : 2 * g + 2, :]
            )
        wo_raw_gct = wo_raw[:].rearrange("q (g t c) -> q g c t", g=PASSES, t=PACK)
        wo_grouped_gct = wo_grouped[:].rearrange("q (g c t) -> q g c t", g=PASSES, t=PACK)
        for g in range(PASSES):
            nc.vector.tensor_copy(out=wo_grouped_gct[:, g], in_=wo_raw_gct[:, g])
        for g in range(PASSES):
            nc.vector.quantize_mx(
                out=wo_codes[:, g * D_OUT : (g + 1) * D_OUT].bitcast(FP8X4),
                scales=wo_scales[:, g * D_OUT : (g + 1) * D_OUT],
                in_=wo_grouped[:, g * D_OUT * PACK : (g + 1) * D_OUT * PACK],
            )

        h_in, bo_in, x_in = {}, {}, {}
        h_grouped, h_codes, h_scales = {}, {}, {}
        acc_of = {}

        def chunk_cols(c, width):
            half = c % CHUNKS_PER_BATCH
            return slice(half * width, (half + 1) * width)

        def load(c):
            b = c // CHUNKS_PER_BATCH
            h_sb = h_pool.tile([P, CHUNK_K], BF16)
            nc.sync.dma_start(out=h_sb[:], in_=h_view[:, b, chunk_cols(c, CHUNK_K)])
            bo_sb = add_pool.tile([P, CHUNK_D], BF16)
            nc.sync.dma_start(out=bo_sb[:], in_=bo_view[:, b, chunk_cols(c, CHUNK_D)])
            x_sb = add_pool.tile([P, CHUNK_D], BF16)
            nc.sync.dma_start(out=x_sb[:], in_=x_view[:, b, chunk_cols(c, CHUNK_D)])
            h_in[c], bo_in[c], x_in[c] = h_sb, bo_sb, x_sb

        def transpose(c):
            h_words = h_in[c][:].bitcast(F32)
            grouped = grouped_pool.tile([P, CHUNK_K], BF16, align_bytes=64)
            grouped_words = grouped[:].bitcast(F32)
            for j in range(CHUNK_TILES):
                xt = psum_xt.tile([P, PLANES, P], F32)
                for a in range(PLANES):
                    first = (j * PLANES + a) * P
                    nc.tensor.transpose(xt[:, a, :], h_words[:, first : first + P], ident[:])
                nc.scalar.copy(
                    out=grouped_words[:, j * WORDS : (j + 1) * WORDS].rearrange(
                        "q (g r u) -> q g r u", g=PASSES, u=2
                    ),
                    in_=xt[:].rearrange("q (g u) r -> q g r u", g=PASSES),
                )
            h_grouped[c] = grouped

        def quantise(c):
            codes = mx_pool.tile([P, CHUNK_TILES * TILE_CODES], U32, align_bytes=64)
            scales = mx_pool.tile([P, CHUNK_TILES * TILE_CODES], U8, align_bytes=64)
            nc.vector.quantize_mx(
                out=codes[:].bitcast(FP8X4), scales=scales[:], in_=h_grouped[c][:]
            )
            h_codes[c], h_scales[c] = codes, scales

        def project(c):
            for j in range(CHUNK_TILES):
                acc = psum_acc.tile([P, D_OUT], F32)
                for g in range(PASSES):
                    tokens = slice((j * PASSES + g) * P, (j * PASSES + g + 1) * P)
                    features = slice(g * D_OUT, (g + 1) * D_OUT)
                    nc.tensor.matmul_mx(
                        out=acc[:],
                        lhsT=h_codes[c][:, tokens].bitcast(FP8X4),
                        lhsT_scale=h_scales[c][:, tokens],
                        rhs=wo_codes[:, features].bitcast(FP8X4),
                        rhs_scale=wo_scales[:, features],
                        start=(g == 0),
                        stop=(g == PASSES - 1),
                    )
                acc_of[(c, j)] = acc

        def add_bias_and_residual(c):
            o_chunk = o_tiles[c // CHUNKS_PER_BATCH][:, chunk_cols(c, CHUNK_D)]
            plain_tiles = CHUNK_TILES if c < TENSOR_ADD_FROM else CHUNK_TILES - TENSOR_ADD_TILES
            if c < GPSIMD_ADD_FROM:
                nc.vector.tensor_tensor(out=o_chunk, in0=bo_in[c][:], in1=x_in[c][:], op=ADD)
            else:
                for j in range(plain_tiles):
                    cols = slice(j * D_OUT, (j + 1) * D_OUT)
                    nc.gpsimd.tensor_tensor(
                        out=o_chunk[:, cols], in0=bo_in[c][:, cols], in1=x_in[c][:, cols], op=ADD
                    )
            for j in range(plain_tiles, CHUNK_TILES):
                cols = slice(j * D_OUT, (j + 1) * D_OUT)
                bx = psum_plain.tile([P, D_OUT], F32, tag="plain")
                nc.tensor.matmul(bx[:], lhsT=ident_bf16[:], rhs=bo_in[c][:, cols], start=True, stop=False)
                nc.tensor.matmul(bx[:], lhsT=ident_bf16[:], rhs=x_in[c][:, cols], start=False, stop=True)
                nc.scalar.copy(out=o_chunk[:, cols], in_=bx[:])

        def add_projection(c):
            o_chunk = o_tiles[c // CHUNKS_PER_BATCH][:, chunk_cols(c, CHUNK_D)]
            for j in range(CHUNK_TILES):
                o_tile = o_chunk[:, j * D_OUT : (j + 1) * D_OUT]
                column = c * CHUNK_TILES + j
                nc.vector.scalar_tensor_tensor(
                    out=o_tile,
                    in0=acc_of[(c, j)][:],
                    scalar=0.0,
                    in1=o_tile,
                    op0=ADD,
                    op1=ADD,
                    accum_out=tile_sums[:, column : column + 1],
                )

        def mean(b):
            columns = slice(b * TILES_PER_BATCH, (b + 1) * TILES_PER_BATCH)
            totals = psum_plain.tile([P, TILES_PER_BATCH], F32, tag="plain")
            nc.tensor.matmul(totals[:], lhsT=ones[:], rhs=tile_sums[:, columns], start=True, stop=True)
            nc.scalar.activation(
                out=mean_scratch[:, columns],
                in_=totals[:],
                func=FUNC.Copy,
                scale=-1.0 / COUNT,
                accum_out=neg_mean[:, b : b + 1],
            )

        def square_tile(c, j):
            b = c // CHUNKS_PER_BATCH
            first = (c % CHUNKS_PER_BATCH) * CHUNK_D + j * D_OUT
            column = c * CHUNK_TILES + j
            squares = scratch_pool.tile([P, D_OUT], BF16)
            nc.scalar.activation(
                out=squares[:],
                in_=o_tiles[b][:, first : first + D_OUT],
                func=FUNC.Square,
                bias=neg_mean[:, b : b + 1],
                accum_out=square_sums[:, column : column + 1],
            )

        def standard_deviation(b):
            columns = slice(b * TILES_PER_BATCH, (b + 1) * TILES_PER_BATCH)
            totals = psum_plain.tile([P, TILES_PER_BATCH], F32, tag="plain")
            nc.tensor.matmul(totals[:], lhsT=ones[:], rhs=square_sums[:, columns], start=True, stop=True)
            nc.scalar.activation(
                out=var_scratch[:, columns],
                in_=totals[:],
                func=FUNC.Copy,
                scale=1.0 / COUNT,
                accum_out=var[:, b : b + 1],
            )
            nc.scalar.activation(out=std[:, b : b + 1], in_=var[:, b : b + 1], func=FUNC.Sqrt, bias=eps[:])

        def normalise_and_store(c):
            b = c // CHUNKS_PER_BATCH
            if c % CHUNKS_PER_BATCH == 0:
                nc.vector.reciprocal(out=rstd[:, b : b + 1], in_=std[:, b : b + 1])
            first = (c % CHUNKS_PER_BATCH) * CHUNK_D
            pieces = [slice(first + n * PIECE_D, first + (n + 1) * PIECE_D) for n in range(NORM_PIECES)]
            for piece in pieces:
                nc.vector.scalar_tensor_tensor(
                    out=o_tiles[b][:, piece],
                    in0=o_tiles[b][:, piece],
                    scalar=neg_mean[:, b : b + 1],
                    in1=gamma_sb[:, piece],
                    op0=ADD,
                    op1=MULT,
                )
            for piece in pieces:
                nc.vector.scalar_tensor_tensor(
                    out=o_tiles[b][:, piece],
                    in0=o_tiles[b][:, piece],
                    scalar=rstd[:, b : b + 1],
                    in1=beta_sb[:, piece],
                    op0=MULT,
                    op1=ADD,
                )
                nc.sync.dma_start(out=out_view[:, b, piece], in_=o_tiles[b][:, piece])

        def is_chunk(c):
            return 0 <= c < CHUNKS

        for c in range(INPUT_BUFS):
            load(c)
        nc.sync.dma_start(out=gamma_sb[:], in_=gamma_view)
        nc.sync.dma_start(out=beta_sb[:], in_=beta_view)
        for c in range(CHUNKS):
            transpose(c)
            quantise(c)
            add_bias_and_residual(c)
            project(c)
            add_projection(c)
            if is_chunk(c + INPUT_BUFS):
                load(c + INPUT_BUFS)
            if c % CHUNKS_PER_BATCH == CHUNKS_PER_BATCH - 1:
                b = c // CHUNKS_PER_BATCH
                mean(b)
                for cc in range(c - CHUNKS_PER_BATCH + 1, c + 1):
                    for j in range(CHUNK_TILES):
                        square_tile(cc, j)
                standard_deviation(b)
        for c in range(CHUNKS):
            normalise_and_store(c)
